import numpy as np
import ml_dtypes


def mxq(x, axis, fmt="e4m3"):
    dtype, down = {"e4m3": (ml_dtypes.float8_e4m3fn, 7), "e5m2": (ml_dtypes.float8_e5m2, 14)}[fmt]
    v = np.moveaxis(np.asarray(x, np.float32).astype(ml_dtypes.bfloat16).astype(np.float64), axis, -1)
    blocks = v.reshape(v.shape[:-1] + (-1, 32))
    amax = np.abs(blocks).max(-1, keepdims=True)
    byte = np.maximum(np.where(amax > 0, np.frexp(amax)[1] - 1 + 127, 0) - down, 1)
    scale = np.exp2(byte - 127.0)
    codes = (blocks / scale).astype(np.float32).astype(dtype).astype(np.float64)
    return np.moveaxis((codes * scale).reshape(v.shape), -1, axis)


WIDE = False


def mx_kscale(k):
    if not WIDE:
        return np.ones(k)
    levels = np.array([18, -18])
    if k % 512:
        return np.exp2(np.random.permutation(np.resize(levels, k // 32))).repeat(32)
    a = np.empty((k // 512, 16))
    for p in range(k // 512):
        a[p, :8] = np.random.permutation(np.resize(levels, 8))
        for g in range(8):
            far = levels[np.abs(levels - a[p, g]) >= 10]
            a[p, g + 8] = far[np.random.randint(len(far))]
    return np.exp2(a.ravel()).repeat(32)


BF16 = ml_dtypes.bfloat16


def bf(x):
    return np.asarray(x, np.float32).astype(BF16)


def f64(x):
    return np.asarray(x).astype(np.float64)


D, KW, STRIDE, STACK, B, O = 32, 11, 3, 16, 1024, 512
W_IN = D * D
POS = (D - KW) // STRIDE + 1
K = STACK * POS * POS


def build_mask():
    base_new = np.tile(np.arange(KW), KW)
    addition_new = np.repeat(np.arange(KW) * D, KW)
    index_1 = addition_new + base_new
    index_width = np.tile(index_1, POS)
    addition_width = np.repeat(STRIDE * np.arange(POS), KW * KW)
    index_row = index_width + addition_width
    index_column = np.tile(index_row, POS)
    addition_height = np.repeat(STRIDE * D * np.arange(POS), KW * KW * POS)
    index_final = index_column + addition_height
    stack = np.repeat(np.arange(POS * POS), KW * KW)
    block = np.zeros((POS * POS, W_IN))
    block[stack, index_final] = 1.0
    return np.vstack([block] * STACK)


def setup_inputs():
    s = mx_kscale(B)[:, None]
    u = mx_kscale(O)
    v = mx_kscale(K)
    z0 = bf(np.random.standard_normal((B, W_IN)))
    T3_0 = bf(np.random.standard_normal((K, W_IN)) * 0.7 / np.sqrt(KW * KW))
    mask = bf(build_mask())
    x1 = bf(np.random.standard_normal((B, K)) * 0.7)
    x2 = bf(np.random.standard_normal((B, K)) * 1.4)
    C_w0 = bf(np.random.standard_normal((O, K)) / np.sqrt(K))
    C_b = bf(np.random.standard_normal(O) * 0.5)
    g = bf(np.random.standard_normal((B, O)) * np.exp2(np.random.randint(-6, 1, (B, 1))) * 2.0 / s * u)
    p3 = f64(z0) @ (f64(mask) * f64(T3_0)).T
    return {"z": bf(f64(z0) * s),
            "T3": bf(f64(T3_0) / v[:, None]),
            "mask": mask,
            "x1": x1,
            "x2": x2,
            "C_w": bf(f64(C_w0) * v / u[:, None]),
            "C_b": C_b,
            "p3": np.asarray(p3, np.float32),
            "grad_out": g}


def reference(z, T3, mask, x1, x2, C_w, C_b, p3, grad_out):
    m = f64(mask)
    dx3 = mxq(f64(grad_out), 1, "e5m2") @ mxq(f64(C_w), 0, "e4m3")
    dp3 = 2.0 * f64(x2) * dx3
    dz = mxq(dp3, 1, "e5m2") @ mxq(m * f64(T3), 0, "e4m3")
    dw = mxq(dp3, 0, "e5m2").T @ mxq(f64(z), 0, "e4m3")
    return dz, m * dw

@@ -1,0 +1,313 @@
+from contextlib import ExitStack
+
+import concourse.mybir as mybir
+from concourse.masks import make_identity
+
+F32 = mybir.dt.float32
+BF16 = mybir.dt.bfloat16
+U32 = mybir.dt.uint32
+U8 = mybir.dt.uint8
+E4M3 = mybir.dt.float8_e4m3fn_x4
+E5M2 = mybir.dt.float8_e5m2_x4
+MULT = mybir.AluOpType.mult
+
+P = 128
+B, O, K, W = 1024, 512, 1024, 1024
+GROUPS = 2
+T = 4
+SPAN = 640
+WIN2 = 448
+WIN1 = 352
+
+FLOPS = 2 * (B * O * K + 2 * B * K * W)
+BYTES = 2 * (4 * 1024 * 1024 + 2 * 512 * 1024) + 4 * 2 * 1024 * 1024
+
+
+def tile_chebyshev_l3_sparsed32_stack_pb_v_kernel(
+    tc, z, T3, mask, x1, x2, C_w, C_b, p3, grad_out, out_0, out_1
+):
+    nc = tc.nc
+    with ExitStack() as ctx:
+        keep = ctx.enter_context(tc.tile_pool(name="keep", bufs=1))
+        stage = ctx.enter_context(tc.tile_pool(name="stage", bufs=3))
+        psum_t = ctx.enter_context(tc.psum_pool(name="psum_t", bufs=2))
+        psum_d = ctx.enter_context(tc.psum_pool(name="psum_d", bufs=3))
+        psum_o = ctx.enter_context(tc.psum_pool(name="psum_o", bufs=3))
+
+        cw_raw = [keep.tile([P, T, 512], BF16, name="cw_raw%d" % c) for c in range(2)]
+        g_raw = [keep.tile([P, T, O], BF16, name="g_raw%d" % g) for g in range(GROUPS)]
+        x2_raw = [keep.tile([P, T, K], BF16, name="x2_raw%d" % g) for g in range(GROUPS)]
+        z_raw = [keep.tile([P, T, W], BF16, name="z_raw%d" % g) for g in range(GROUPS)]
+        t3_raw = [keep.tile([P, T, SPAN], BF16, name="t3_raw%d" % h) for h in range(2)]
+        mask_t = keep.tile([P, T, SPAN], BF16, name="mask_t")
+        mask_o = keep.tile([P, WIN1], BF16, name="mask_o")
+        ident = keep.tile([P, P], F32, name="ident")
+        zeros = keep.tile([P, 672], F32, name="zeros")
+
+        cw_il = keep.tile([P, 2, 512, T], BF16, name="cw_il", align_bytes=64)
+        cw_codes = keep.tile([P, 2, 512], U32, name="cw_codes", align_bytes=64)
+        cw_scales = keep.tile([P, 2, 512], U8, name="cw_scales", align_bytes=64)
+        g_il = [keep.tile([P, T, P, 2], F32, name="g_il%d" % g, align_bytes=64) for g in range(GROUPS)]
+        g_codes = [keep.tile([P, T, P], U32, name="g_codes%d" % g, align_bytes=64) for g in range(GROUPS)]
+        g_scales = [keep.tile([P, T, P], U8, name="g_scales%d" % g, align_bytes=64) for g in range(GROUPS)]
+        m_il = [keep.tile([P, SPAN, T], BF16, name="m_il%d" % h, align_bytes=64) for h in range(2)]
+        m_codes = [keep.tile([P, W], U32, name="m_codes%d" % h, align_bytes=64) for h in range(2)]
+        m_scales = [keep.tile([P, W], U8, name="m_scales%d" % h, align_bytes=64) for h in range(2)]
+        dp = [keep.tile([P, T, K], BF16, name="dp%d" % g) for g in range(GROUPS)]
+        dpt_codes = [keep.tile([P, T, 2, P], U32, name="dpt_codes%d" % g, align_bytes=64) for g in range(GROUPS)]
+        dpt_scales = [keep.tile([P, T, 2, P], U8, name="dpt_scales%d" % g, align_bytes=64) for g in range(GROUPS)]
+        dpa_il = [keep.tile([P, K, T], BF16, name="dpa_il%d" % g, align_bytes=64) for g in range(GROUPS)]
+        dpa_codes = [keep.tile([P, K], U32, name="dpa_codes%d" % g, align_bytes=64) for g in range(GROUPS)]
+        dpa_scales = [keep.tile([P, K], U8, name="dpa_scales%d" % g, align_bytes=64) for g in range(GROUPS)]
+        z_il = [keep.tile([P, W, T], BF16, name="z_il%d" % g, align_bytes=64) for g in range(GROUPS)]
+        z_codes = [keep.tile([P, W], U32, name="z_codes%d" % g, align_bytes=64) for g in range(GROUPS)]
+        z_scales = [keep.tile([P, W], U8, name="z_scales%d" % g, align_bytes=64) for g in range(GROUPS)]
+
+        cw_v = C_w.rearrange("(p j) k -> p j k", j=T)
+        g_v = grad_out.rearrange("(g p j) o -> g p j o", g=GROUPS, j=T)
+        x2_v = x2.rearrange("(g p j) k -> g p j k", g=GROUPS, j=T)
+        z_v = z.rearrange("(g p j) w -> g p j w", g=GROUPS, j=T)
+        t3_v = T3.rearrange("(s c q e) w -> c e s q w", s=16, c=4, q=8, e=2)
+        mask_v = mask.rearrange("(s c q e) w -> c e s q w", s=16, c=4, q=8, e=2)
+        mask_i = mask.rearrange("(s i j) w -> i s j w", s=16, i=8, j=8)
+        out0_v = out_0.rearrange("(g p t) w -> g t p w", g=GROUPS, t=T)
+        out1_v = out_1.rearrange("(s i j) w -> i s j w", s=16, i=8, j=8)
+
+        def load_cw(c):
+            nc.sync.dma_start(out=cw_raw[c][:], in_=cw_v[:, :, 512 * c : 512 * (c + 1)])
+
+        def load_t3(h):
+            for u in range(2):
+                for e in range(2):
+                    col = 192 * (2 * h + u)
+                    nc.sync.dma_start(
+                        out=t3_raw[h][:, 2 * u + e, 192 * u : 192 * u + WIN2],
+                        in_=t3_v[2 * h + u, e, :, :, col : col + WIN2],
+                    )
+
+        for u in range(2):
+            for e in range(2):
+                nc.sync.dma_start(
+                    out=mask_t[:, 2 * u + e, 192 * u : 192 * u + WIN2], in_=mask_v[0, e, :, :, 0:WIN2]
+                )
+        load_t3(0)
+        nc.sync.dma_start(out=g_raw[0][:], in_=g_v[0])
+        load_cw(0)
+        load_t3(1)
+        load_cw(1)
+        nc.sync.dma_start(out=z_raw[0][:], in_=z_v[0])
+        nc.sync.dma_start(out=x2_raw[0][:], in_=x2_v[0])
+        nc.sync.dma_start(out=g_raw[1][:], in_=g_v[1])
+        nc.sync.dma_start(out=x2_raw[1][:], in_=x2_v[1])
+        nc.sync.dma_start(out=z_raw[1][:], in_=z_v[1])
+        nc.sync.dma_start(out=mask_o[:], in_=mask_i[0, :, :, 0:WIN1])
+
+        make_identity(nc, ident[:])
+        for h in range(2):
+            nc.gpsimd.memset(t3_raw[h][:, 0:2, WIN2:SPAN], 0.0)
+            nc.gpsimd.memset(t3_raw[h][:, 2:4, 0:192], 0.0)
+        nc.gpsimd.memset(mask_t[:, 0:2, WIN2:SPAN], 0.0)
+        nc.gpsimd.memset(mask_t[:, 2:4, 0:192], 0.0)
+        for h, (a, b) in enumerate(((SPAN, W), (0, 384))):
+            nc.gpsimd.memset(m_codes[h][:, a:b], 0)
+            nc.gpsimd.memset(m_scales[h][:, a:b].bitcast(U32), 0)
+        nc.gpsimd.memset(zeros[:], 0.0)
+
+        def transpose_g(g, b):
+            ps = psum_t.tile([P, 2, 2, P], F32, name="tp")
+            for a in range(2):
+                words = g_raw[g][:, 2 * b + a, :].bitcast(F32)
+                for u in range(2):
+                    nc.tensor.transpose(ps[:, a, u, :], words[:, u : O // 2 : 2], ident[:])
+            nc.scalar.copy(out=g_il[g][:, 2 * b : 2 * b + 2], in_=ps[:].rearrange("p a u m -> p a m u"))
+
+        def quantize_g(g):
+            nc.vector.quantize_mx(
+                out=g_codes[g][:].rearrange("p t m -> p (t m)").bitcast(E5M2),
+                scales=g_scales[g][:].rearrange("p t m -> p (t m)"),
+                in_=g_il[g][:].rearrange("p t m u -> p (t m u)").bitcast(BF16),
+            )
+
+        def interleave_cw(h, c):
+            src = cw_raw[c][:].rearrange("p j (s h u r) -> p h u s r j", s=8, h=2, u=2, r=16)
+            dst = cw_il[:, h].rearrange("p (u s r) j -> p u s r j", u=2, s=16, r=16)
+            for u in range(2):
+                nc.scalar.activation(
+                    out=dst[:, u, 8 * c : 8 * c + 8],
+                    in_=src[:, h, u],
+                    func=mybir.ActivationFunctionType.Copy,
+                    scale=2.0,
+                )
+
+        def quantize_cw(h):
+            nc.vector.quantize_mx(
+                out=cw_codes[:, h, :].bitcast(E4M3),
+                scales=cw_scales[:, h, :],
+                in_=cw_il[:, h].rearrange("p n j -> p (n j)"),
+            )
+
+        def dx3(g, t, h):
+            ps = psum_d.tile([P, 512], F32, name="dx")
+            nc.tensor.matmul_mx(
+                out=ps[:],
+                lhsT=g_codes[g][:, t, :].bitcast(E5M2),
+                lhsT_scale=g_scales[g][:, t, :],
+                rhs=cw_codes[:, h, :].bitcast(E4M3),
+                rhs_scale=cw_scales[:, h, :],
+                start=True,
+                stop=True,
+            )
+            x2_p = x2_raw[g][:, t, :].rearrange("p (s h u r) -> p h u s r", s=16, h=2, u=2, r=16)
+            nc.vector.tensor_tensor(
+                out=dp[g][:, t, 512 * h : 512 * (h + 1)].rearrange("p (u s r) -> p u s r", u=2, r=16),
+                in0=ps[:].rearrange("p (u s r) -> p u s r", u=2, r=16),
+                in1=x2_p[:, h],
+                op=MULT,
+            )
+
+        def transpose_dp(g, t):
+            ps = psum_t.tile([P, 2, 2, P], F32, name="tp")
+            words = dp[g][:, t, :].bitcast(F32)
+            for h in range(2):
+                for u in range(2):
+                    n = 128 * (2 * h + u)
+                    nc.tensor.transpose(ps[:, h, u, :], words[:, n : n + 128], ident[:])
+            il = stage.tile([P, 2, P, 2], F32, name="dpt_il", align_bytes=64)
+            nc.scalar.copy(out=il[:], in_=ps[:].rearrange("p h u m -> p h m u"))
+            nc.vector.quantize_mx(
+                out=dpt_codes[g][:, t].rearrange("p h m -> p (h m)").bitcast(E5M2),
+                scales=dpt_scales[g][:, t].rearrange("p h m -> p (h m)"),
+                in_=il[:].rearrange("p h m u -> p (h m u)").bitcast(BF16),
+            )
+
+        def mask_t3(h):
+            nc.vector.tensor_tensor(
+                out=m_il[h][:].rearrange("p (c i) t -> p c t i", i=4),
+                in0=t3_raw[h][:].rearrange("p t (c i) -> p c t i", i=4),
+                in1=mask_t[:].rearrange("p t (c i) -> p c t i", i=4),
+                op=MULT,
+            )
+
+        def quantize_m(h):
+            for a, n in ((0, 512), (512, 128)):
+                col = 384 * h + a
+                nc.vector.quantize_mx(
+                    out=m_codes[h][:, col : col + n].bitcast(E4M3),
+                    scales=m_scales[h][:, col : col + n],
+                    in_=m_il[h][:, a : a + n, :].rearrange("p n t -> p (n t)"),
+                )
+
+        def product_0(g, t):
+            res = stage.tile([P, W], F32, name="res0")
+            for w in range(2):
+                ps = psum_o.tile([P, 512], F32, name="po")
+                for h in range(2):
+                    nc.tensor.matmul_mx(
+                        out=ps[:],
+                        lhsT=dpt_codes[g][:, t, h, :].bitcast(E5M2),
+                        lhsT_scale=dpt_scales[g][:, t, h, :],
+                        rhs=m_codes[h][:, 512 * w : 512 * (w + 1)].bitcast(E4M3),
+                        rhs_scale=m_scales[h][:, 512 * w : 512 * (w + 1)],
+                        start=(h == 0),
+                        stop=(h == 1),
+                    )
+                nc.scalar.copy(out=res[:, 512 * w : 512 * (w + 1)], in_=ps[:])
+            nc.sync.dma_start(out=out0_v[g, t], in_=res[:])
+
+        def interleave_dp(g, i, copy):
+            hu, lo = i // 2, i % 2
+            src = dp[g][:].rearrange("p t (c s l q i) -> p c l s q t i", c=4, s=16, l=2, q=2, i=4)
+            dst = dpa_il[g][:, 128 * i : 128 * (i + 1), :].rearrange("p (s q i) t -> p s q t i", s=16, q=2, i=4)
+            copy(out=dst, in_=src[:, hu, lo])
+
+        def quantize_dp(g, h):
+            n = slice(512 * h, 512 * (h + 1))
+            nc.vector.quantize_mx(
+                out=dpa_codes[g][:, n].bitcast(E5M2),
+                scales=dpa_scales[g][:, n],
+                in_=dpa_il[g][:, n, :].rearrange("p n t -> p (n t)"),
+            )
+
+        def interleave_z(g, b, copy):
+            n = slice(512 * b, 512 * (b + 1))
+            copy(
+                out=z_il[g][:, n, :].rearrange("p (c i) t -> p c t i", i=4),
+                in_=z_raw[g][:, :, n].rearrange("p t (c i) -> p c t i", i=4),
+            )
+
+        def quantize_z(g, b):
+            n = slice(512 * b, 512 * (b + 1))
+            nc.vector.quantize_mx(
+                out=z_codes[g][:, n].bitcast(E4M3),
+                scales=z_scales[g][:, n],
+                in_=z_il[g][:, n, :].rearrange("p n t -> p (n t)"),
+            )
+
+        def product_1(i):
+            first = 96 * i
+            base = min(first // 64 * 64, W - 512)
+            ps = psum_o.tile([P, 512], F32, name="po")
+            for g in range(GROUPS):
+                nc.tensor.matmul_mx(
+                    out=ps[:],
+                    lhsT=dpa_codes[g][:, 128 * i : 128 * (i + 1)].bitcast(E5M2),
+                    lhsT_scale=dpa_scales[g][:, 128 * i : 128 * (i + 1)],
+                    rhs=z_codes[g][:, base : base + 512].bitcast(E4M3),
+                    rhs_scale=z_scales[g][:, base : base + 512],
+                    start=(g == 0),
+                    stop=(g == GROUPS - 1),
+                )
+            res = stage.tile([P, WIN1], F32, name="res1")
+            nc.vector.tensor_tensor(
+                out=res[:], in0=ps[:, first - base : first - base + WIN1], in1=mask_o[:], op=MULT
+            )
+            nc.sync.dma_start(out=out1_v[i, :, :, first : first + WIN1], in_=res[:])
+
+        def zero_1(i):
+            left, right = 96 * i, 672 - 96 * i
+            if left > 0:
+                nc.sync.dma_start(out=out1_v[i, :, :, 0:left], in_=zeros[:, 0:left])
+            if right > 0:
+                nc.sync.dma_start(out=out1_v[i, :, :, left + WIN1 : W], in_=zeros[:, 0:right])
+
+        vcopy, scopy = nc.vector.tensor_copy, nc.scalar.copy
+
+        mask_t3(0)
+        quantize_m(0)
+        transpose_g(0, 0)
+        transpose_g(0, 1)
+        quantize_g(0)
+        for c in range(2):
+            for h in range(2):
+                interleave_cw(h, c)
+        for h in range(2):
+            quantize_cw(h)
+        mask_t3(1)
+        quantize_m(1)
+        transpose_g(1, 0)
+        transpose_g(1, 1)
+        quantize_g(1)
+        steps = [(g, t) for g in range(GROUPS) for t in range(T)]
+        for n, (g, t) in enumerate(steps):
+            dx3(g, t, 0)
+            dx3(g, t, 1)
+            transpose_dp(g, t)
+            if n > 0:
+                product_0(*steps[n - 1])
+        for i in range(8):
+            interleave_dp(0, i, vcopy)
+        for h in range(2):
+            quantize_dp(0, h)
+        for g in range(GROUPS):
+            for b in range(2):
+                interleave_z(g, b, scopy)
+                quantize_z(g, b)
+        for i in range(8):
+            interleave_dp(1, i, vcopy if i < 4 else scopy)
+        for h in range(2):
+            quantize_dp(1, h)
+        for i in range(8):
+            product_1(i)
+        product_0(*steps[-1])
+        for i in range(8):
+            zero_1(i)

@@ -10,6 +10,7 @@ U8 = mybir.dt.uint8
 E4M3 = mybir.dt.float8_e4m3fn_x4
 E5M2 = mybir.dt.float8_e5m2_x4
 MULT = mybir.AluOpType.mult
+COPY = mybir.ActivationFunctionType.Copy
 
 P = 128
 B, O, K, W = 1024, 512, 1024, 1024
@@ -22,6 +23,20 @@ WIN1 = 352
 FLOPS = 2 * (B * O * K + 2 * B * K * W)
 BYTES = 2 * (4 * 1024 * 1024 + 2 * 512 * 1024) + 4 * 2 * 1024 * 1024
 
+ORDER = """
+G0 CwA CwB x20 G1 z1 m1 mask T30 GT01 GT00 GC01 GC00 T31 CI1A0:V CI1A1:V CI0A0:S GQ0 CI0A1:S z0
+CI1B1:V CI1B0:S CI0B1:V CI0B0:S CQ1 CQ0 DX031 ZR7 DX011 M031 DX001 M011 DX000 ZR1 GT10 M001 DX020
+GC10 M000 GT11 DX030 M020 GC11 DX010 TT00 M030 ZR4 ZI13:S x21 DX021 ZI10:V TT03 M010 TC00 ZR5 M021
+TC03 TT01 TQ00 AI00:S TT02 GQ1 ZR3 TC01 MT0 DX121 TC02 DX110 DX130 ZI12:S ZR0 AI07:S TQ02 MQ0a
+ZI11:S ZR6 ZQ11 MT1 ZI02:S ZR2 ZI00:S TQ01 AI01:S MQ1 MQ1a AI03:S MQ0 ZQ10 O021 AI05:S TQ03 O010
+OC021 M121 O031 OC010 M110 O000 OC031 M130 O020 OC000 ZI01:V O001 OC020 ZI03:V O030 OC001 ST02 ZQ00
+DX100 OC030 ST00 O011 ZQ01 ST03 DX111 OC011 DX131 M100 ST01 M111 DX101 M131 TT11 M101 DX120 TC11
+TT13 AI06:V TT10 TC13 TQ11 AI15:V O111 TC10 TQ13 O110 AI14:V OC111 TQ10 O131 OC110 AI16:V AI17:V
+O100 OC131 ST11 AI04:V O101 OC100 AQ11 O130 OC101 AQ01 OC130 ST10 M120 P7 ST13 AI02:V TT12 AI13:S
+OM7 P6 TC12 AQ00 SW7 P5 AI12:S OM6 P4 TQ12 AI10:S SW6 OM5 O121 AI11:S OM4 SW5 O120 SW4 OC121 AQ10
+OC120 P0 ST12 P1 OM0 P2 SW0 OM1 P3 SW1 OM2 SW2 OM3 SW3
+""".split()
+
 
 def tile_chebyshev_l3_sparsed32_stack_pb_v_kernel(
     tc, z, T3, mask, x1, x2, C_w, C_b, p3, grad_out, out_0, out_1
@@ -29,7 +44,8 @@ def tile_chebyshev_l3_sparsed32_stack_pb_v_kernel(
     nc = tc.nc
     with ExitStack() as ctx:
         keep = ctx.enter_context(tc.tile_pool(name="keep", bufs=1))
-        stage = ctx.enter_context(tc.tile_pool(name="stage", bufs=3))
+        stage = ctx.enter_context(tc.tile_pool(name="stage", bufs=4))
+        stage0 = ctx.enter_context(tc.tile_pool(name="stage0", bufs=5))
         psum_t = ctx.enter_context(tc.psum_pool(name="psum_t", bufs=2))
         psum_d = ctx.enter_context(tc.psum_pool(name="psum_d", bufs=3))
         psum_o = ctx.enter_context(tc.psum_pool(name="psum_o", bufs=3))
@@ -67,79 +83,82 @@ def tile_chebyshev_l3_sparsed32_stack_pb_v_kernel(
         g_v = grad_out.rearrange("(g p j) o -> g p j o", g=GROUPS, j=T)
         x2_v = x2.rearrange("(g p j) k -> g p j k", g=GROUPS, j=T)
         z_v = z.rearrange("(g p j) w -> g p j w", g=GROUPS, j=T)
-        t3_v = T3.rearrange("(s c q e) w -> c e s q w", s=16, c=4, q=8, e=2)
-        mask_v = mask.rearrange("(s c q e) w -> c e s q w", s=16, c=4, q=8, e=2)
+        t3_v = T3.rearrange("(s c r) w -> c s r w", s=16, c=4, r=16)
+        mask_v = mask.rearrange("(s c r) w -> c s r w", s=16, c=4, r=16)
         mask_i = mask.rearrange("(s i j) w -> i s j w", s=16, i=8, j=8)
         out0_v = out_0.rearrange("(g p t) w -> g t p w", g=GROUPS, t=T)
         out1_v = out_1.rearrange("(s i j) w -> i s j w", s=16, i=8, j=8)
+
+        psum = {}
+        sbuf = {}
+
+        def copy(engine, out, in_):
+            if engine == "V":
+                nc.vector.tensor_copy(out=out, in_=in_)
+            else:
+                nc.scalar.copy(out=out, in_=in_)
 
         def load_cw(c):
             nc.sync.dma_start(out=cw_raw[c][:], in_=cw_v[:, :, 512 * c : 512 * (c + 1)])
 
         def load_t3(h):
             for u in range(2):
-                for e in range(2):
-                    col = 192 * (2 * h + u)
-                    nc.sync.dma_start(
-                        out=t3_raw[h][:, 2 * u + e, 192 * u : 192 * u + WIN2],
-                        in_=t3_v[2 * h + u, e, :, :, col : col + WIN2],
-                    )
-
-        for u in range(2):
-            for e in range(2):
+                col = 192 * (2 * h + u)
                 nc.sync.dma_start(
-                    out=mask_t[:, 2 * u + e, 192 * u : 192 * u + WIN2], in_=mask_v[0, e, :, :, 0:WIN2]
+                    out=t3_raw[h][:, 2 * u : 2 * u + 2, 192 * u : 192 * u + WIN2],
+                    in_=t3_v[2 * h + u, :, :, col : col + WIN2],
                 )
-        load_t3(0)
-        nc.sync.dma_start(out=g_raw[0][:], in_=g_v[0])
-        load_cw(0)
-        load_t3(1)
-        load_cw(1)
-        nc.sync.dma_start(out=z_raw[0][:], in_=z_v[0])
-        nc.sync.dma_start(out=x2_raw[0][:], in_=x2_v[0])
-        nc.sync.dma_start(out=g_raw[1][:], in_=g_v[1])
-        nc.sync.dma_start(out=x2_raw[1][:], in_=x2_v[1])
-        nc.sync.dma_start(out=z_raw[1][:], in_=z_v[1])
-        nc.sync.dma_start(out=mask_o[:], in_=mask_i[0, :, :, 0:WIN1])
 
-        make_identity(nc, ident[:])
-        for h in range(2):
-            nc.gpsimd.memset(t3_raw[h][:, 0:2, WIN2:SPAN], 0.0)
-            nc.gpsimd.memset(t3_raw[h][:, 2:4, 0:192], 0.0)
-        nc.gpsimd.memset(mask_t[:, 0:2, WIN2:SPAN], 0.0)
-        nc.gpsimd.memset(mask_t[:, 2:4, 0:192], 0.0)
-        for h, (a, b) in enumerate(((SPAN, W), (0, 384))):
-            nc.gpsimd.memset(m_codes[h][:, a:b], 0)
-            nc.gpsimd.memset(m_scales[h][:, a:b].bitcast(U32), 0)
-        nc.gpsimd.memset(zeros[:], 0.0)
+        def load_mask():
+            for u in range(2):
+                nc.sync.dma_start(
+                    out=mask_t[:, 2 * u : 2 * u + 2, 192 * u : 192 * u + WIN2], in_=mask_v[0, :, :, 0:WIN2]
+                )
 
-        def transpose_g(g, b):
+        def load_mask_o():
+            nc.sync.dma_start(out=mask_o[:], in_=mask_i[0, :, :, 0:WIN1])
+
+        def store_0(g, t):
+            nc.sync.dma_start(out=out0_v[g, t], in_=sbuf["res0", g, t][:])
+
+        def store_1(i):
+            first = 96 * i
+            nc.sync.dma_start(out=out1_v[i, :, :, first : first + WIN1], in_=sbuf["res1", i][:])
+
+        def zero_1(i):
+            left, right = 96 * i, 672 - 96 * i
+            if left > 0:
+                nc.sync.dma_start(out=out1_v[i, :, :, 0:left], in_=zeros[:, 0:left])
+            if right > 0:
+                nc.sync.dma_start(out=out1_v[i, :, :, left + WIN1 : W], in_=zeros[:, 0:right])
+
+        def g_transpose(g, b):
             ps = psum_t.tile([P, 2, 2, P], F32, name="tp")
             for a in range(2):
                 words = g_raw[g][:, 2 * b + a, :].bitcast(F32)
                 for u in range(2):
                     nc.tensor.transpose(ps[:, a, u, :], words[:, u : O // 2 : 2], ident[:])
-            nc.scalar.copy(out=g_il[g][:, 2 * b : 2 * b + 2], in_=ps[:].rearrange("p a u m -> p a m u"))
+            psum["g", g, b] = ps
 
-        def quantize_g(g):
+        def g_copy(g, b):
+            copy("S", g_il[g][:, 2 * b : 2 * b + 2], psum["g", g, b][:].rearrange("p a u m -> p a m u"))
+
+        def g_quantize(g):
             nc.vector.quantize_mx(
                 out=g_codes[g][:].rearrange("p t m -> p (t m)").bitcast(E5M2),
                 scales=g_scales[g][:].rearrange("p t m -> p (t m)"),
                 in_=g_il[g][:].rearrange("p t m u -> p (t m u)").bitcast(BF16),
             )
 
-        def interleave_cw(h, c):
-            src = cw_raw[c][:].rearrange("p j (s h u r) -> p h u s r j", s=8, h=2, u=2, r=16)
-            dst = cw_il[:, h].rearrange("p (u s r) j -> p u s r j", u=2, s=16, r=16)
-            for u in range(2):
-                nc.scalar.activation(
-                    out=dst[:, u, 8 * c : 8 * c + 8],
-                    in_=src[:, h, u],
-                    func=mybir.ActivationFunctionType.Copy,
-                    scale=2.0,
-                )
+        def cw_copy(h, c, u, engine):
+            src = cw_raw[c][:].rearrange("p j (s h u r) -> p h u s r j", s=8, h=2, u=2, r=16)[:, h, u]
+            dst = cw_il[:, h].rearrange("p (u s r) j -> p u s r j", u=2, s=16, r=16)[:, u, 8 * c : 8 * c + 8]
+            if engine == "V":
+                nc.vector.tensor_scalar(out=dst, in0=src, scalar1=2.0, scalar2=None, op0=MULT)
+            else:
+                nc.scalar.activation(out=dst, in_=src, func=COPY, scale=2.0)
 
-        def quantize_cw(h):
+        def cw_quantize(h):
             nc.vector.quantize_mx(
                 out=cw_codes[:, h, :].bitcast(E4M3),
                 scales=cw_scales[:, h, :],
@@ -157,70 +176,45 @@ def tile_chebyshev_l3_sparsed32_stack_pb_v_kernel(
                 start=True,
                 stop=True,
             )
+            psum["dx", g, t, h] = ps
+
+        def dp3(g, t, h):
             x2_p = x2_raw[g][:, t, :].rearrange("p (s h u r) -> p h u s r", s=16, h=2, u=2, r=16)
             nc.vector.tensor_tensor(
                 out=dp[g][:, t, 512 * h : 512 * (h + 1)].rearrange("p (u s r) -> p u s r", u=2, r=16),
-                in0=ps[:].rearrange("p (u s r) -> p u s r", u=2, r=16),
+                in0=psum["dx", g, t, h][:].rearrange("p (u s r) -> p u s r", u=2, r=16),
                 in1=x2_p[:, h],
                 op=MULT,
             )
 
-        def transpose_dp(g, t):
+        def dpt_transpose(g, t):
             ps = psum_t.tile([P, 2, 2, P], F32, name="tp")
             words = dp[g][:, t, :].bitcast(F32)
             for h in range(2):
                 for u in range(2):
                     n = 128 * (2 * h + u)
                     nc.tensor.transpose(ps[:, h, u, :], words[:, n : n + 128], ident[:])
+            psum["dpt", g, t] = ps
+
+        def dpt_copy(g, t):
             il = stage.tile([P, 2, P, 2], F32, name="dpt_il", align_bytes=64)
-            nc.scalar.copy(out=il[:], in_=ps[:].rearrange("p h u m -> p h m u"))
+            copy("S", il[:], psum["dpt", g, t][:].rearrange("p h u m -> p h m u"))
+            sbuf["dpt", g, t] = il
+
+        def dpt_quantize(g, t):
             nc.vector.quantize_mx(
                 out=dpt_codes[g][:, t].rearrange("p h m -> p (h m)").bitcast(E5M2),
                 scales=dpt_scales[g][:, t].rearrange("p h m -> p (h m)"),
-                in_=il[:].rearrange("p h m u -> p (h m u)").bitcast(BF16),
+                in_=sbuf["dpt", g, t][:].rearrange("p h m u -> p (h m u)").bitcast(BF16),
             )
 
-        def mask_t3(h):
-            nc.vector.tensor_tensor(
-                out=m_il[h][:].rearrange("p (c i) t -> p c t i", i=4),
-                in0=t3_raw[h][:].rearrange("p t (c i) -> p c t i", i=4),
-                in1=mask_t[:].rearrange("p t (c i) -> p c t i", i=4),
-                op=MULT,
-            )
-
-        def quantize_m(h):
-            for a, n in ((0, 512), (512, 128)):
-                col = 384 * h + a
-                nc.vector.quantize_mx(
-                    out=m_codes[h][:, col : col + n].bitcast(E4M3),
-                    scales=m_scales[h][:, col : col + n],
-                    in_=m_il[h][:, a : a + n, :].rearrange("p n t -> p (n t)"),
-                )
-
-        def product_0(g, t):
-            res = stage.tile([P, W], F32, name="res0")
-            for w in range(2):
-                ps = psum_o.tile([P, 512], F32, name="po")
-                for h in range(2):
-                    nc.tensor.matmul_mx(
-                        out=ps[:],
-                        lhsT=dpt_codes[g][:, t, h, :].bitcast(E5M2),
-                        lhsT_scale=dpt_scales[g][:, t, h, :],
-                        rhs=m_codes[h][:, 512 * w : 512 * (w + 1)].bitcast(E4M3),
-                        rhs_scale=m_scales[h][:, 512 * w : 512 * (w + 1)],
-                        start=(h == 0),
-                        stop=(h == 1),
-                    )
-                nc.scalar.copy(out=res[:, 512 * w : 512 * (w + 1)], in_=ps[:])
-            nc.sync.dma_start(out=out0_v[g, t], in_=res[:])
-
-        def interleave_dp(g, i, copy):
+        def dpa_copy(g, i, engine):
             hu, lo = i // 2, i % 2
             src = dp[g][:].rearrange("p t (c s l q i) -> p c l s q t i", c=4, s=16, l=2, q=2, i=4)
             dst = dpa_il[g][:, 128 * i : 128 * (i + 1), :].rearrange("p (s q i) t -> p s q t i", s=16, q=2, i=4)
-            copy(out=dst, in_=src[:, hu, lo])
+            copy(engine, dst, src[:, hu, lo])
 
-        def quantize_dp(g, h):
+        def dpa_quantize(g, h):
             n = slice(512 * h, 512 * (h + 1))
             nc.vector.quantize_mx(
                 out=dpa_codes[g][:, n].bitcast(E5M2),
@@ -228,14 +222,32 @@ def tile_chebyshev_l3_sparsed32_stack_pb_v_kernel(
                 in_=dpa_il[g][:, n, :].rearrange("p n t -> p (n t)"),
             )
 
-        def interleave_z(g, b, copy):
-            n = slice(512 * b, 512 * (b + 1))
-            copy(
-                out=z_il[g][:, n, :].rearrange("p (c i) t -> p c t i", i=4),
-                in_=z_raw[g][:, :, n].rearrange("p t (c i) -> p c t i", i=4),
+        def m_multiply(h):
+            for a, b, t0, t1 in ((0, 192, 0, 2), (192, 448, 0, 4), (448, 640, 2, 4)):
+                nc.vector.tensor_tensor(
+                    out=m_il[h][:, a:b, t0:t1].rearrange("p (c i) t -> p c t i", i=4),
+                    in0=t3_raw[h][:, t0:t1, a:b].rearrange("p t (c i) -> p c t i", i=4),
+                    in1=mask_t[:, t0:t1, a:b].rearrange("p t (c i) -> p c t i", i=4),
+                    op=MULT,
+                )
+
+        def m_quantize(h, a, n):
+            col = 384 * h + a
+            nc.vector.quantize_mx(
+                out=m_codes[h][:, col : col + n].bitcast(E4M3),
+                scales=m_scales[h][:, col : col + n],
+                in_=m_il[h][:, a : a + n, :].rearrange("p n t -> p (n t)"),
             )
 
-        def quantize_z(g, b):
+        def z_copy(g, b, engine):
+            n = slice(256 * b, 256 * (b + 1))
+            copy(
+                engine,
+                z_il[g][:, n, :].rearrange("p (c i) t -> p c t i", i=4),
+                z_raw[g][:, :, n].rearrange("p t (c i) -> p c t i", i=4),
+            )
+
+        def z_quantize(g, b):
             n = slice(512 * b, 512 * (b + 1))
             nc.vector.quantize_mx(
                 out=z_codes[g][:, n].bitcast(E4M3),
@@ -243,9 +255,31 @@ def tile_chebyshev_l3_sparsed32_stack_pb_v_kernel(
                 in_=z_il[g][:, n, :].rearrange("p n t -> p (n t)"),
             )
 
+        def product_0(g, t, w):
+            ps = psum_o.tile([P, 512], F32, name="po")
+            for h in range(2):
+                nc.tensor.matmul_mx(
+                    out=ps[:],
+                    lhsT=dpt_codes[g][:, t, h, :].bitcast(E5M2),
+                    lhsT_scale=dpt_scales[g][:, t, h, :],
+                    rhs=m_codes[h][:, 512 * w : 512 * (w + 1)].bitcast(E4M3),
+                    rhs_scale=m_scales[h][:, 512 * w : 512 * (w + 1)],
+                    start=(h == 0),
+                    stop=(h == 1),
+                )
+            psum["o0", g, t, w] = ps
+
+        def result_0(g, t, w):
+            if ("res0", g, t) not in sbuf:
+                res0 = stage0.tile([P, W], F32, name="res0")
+                sbuf["res0", g, t] = res0
+            copy("S", sbuf["res0", g, t][:, 512 * w : 512 * (w + 1)], psum["o0", g, t, w][:])
+
+        def window(i):
+            return min(96 * i // 64 * 64, W - 512)
+
         def product_1(i):
-            first = 96 * i
-            base = min(first // 64 * 64, W - 512)
+            base = window(i)
             ps = psum_o.tile([P, 512], F32, name="po")
             for g in range(GROUPS):
                 nc.tensor.matmul_mx(
@@ -257,57 +291,90 @@ def tile_chebyshev_l3_sparsed32_stack_pb_v_kernel(
                     start=(g == 0),
                     stop=(g == GROUPS - 1),
                 )
-            res = stage.tile([P, WIN1], F32, name="res1")
+            psum["o1", i] = ps
+
+        def result_1(i):
+            first = 96 * i - window(i)
+            res1 = stage.tile([P, WIN1], F32, name="res1")
             nc.vector.tensor_tensor(
-                out=res[:], in0=ps[:, first - base : first - base + WIN1], in1=mask_o[:], op=MULT
+                out=res1[:], in0=psum["o1", i][:, first : first + WIN1], in1=mask_o[:], op=MULT
             )
-            nc.sync.dma_start(out=out1_v[i, :, :, first : first + WIN1], in_=res[:])
+            sbuf["res1", i] = res1
 
-        def zero_1(i):
-            left, right = 96 * i, 672 - 96 * i
-            if left > 0:
-                nc.sync.dma_start(out=out1_v[i, :, :, 0:left], in_=zeros[:, 0:left])
-            if right > 0:
-                nc.sync.dma_start(out=out1_v[i, :, :, left + WIN1 : W], in_=zeros[:, 0:right])
-
-        vcopy, scopy = nc.vector.tensor_copy, nc.scalar.copy
-
-        mask_t3(0)
-        quantize_m(0)
-        transpose_g(0, 0)
-        transpose_g(0, 1)
-        quantize_g(0)
-        for c in range(2):
+        with tc.manual_schedule():
+            make_identity(nc, ident[:])
             for h in range(2):
-                interleave_cw(h, c)
-        for h in range(2):
-            quantize_cw(h)
-        mask_t3(1)
-        quantize_m(1)
-        transpose_g(1, 0)
-        transpose_g(1, 1)
-        quantize_g(1)
-        steps = [(g, t) for g in range(GROUPS) for t in range(T)]
-        for n, (g, t) in enumerate(steps):
-            dx3(g, t, 0)
-            dx3(g, t, 1)
-            transpose_dp(g, t)
-            if n > 0:
-                product_0(*steps[n - 1])
-        for i in range(8):
-            interleave_dp(0, i, vcopy)
-        for h in range(2):
-            quantize_dp(0, h)
-        for g in range(GROUPS):
-            for b in range(2):
-                interleave_z(g, b, scopy)
-                quantize_z(g, b)
-        for i in range(8):
-            interleave_dp(1, i, vcopy if i < 4 else scopy)
-        for h in range(2):
-            quantize_dp(1, h)
-        for i in range(8):
-            product_1(i)
-        product_0(*steps[-1])
-        for i in range(8):
-            zero_1(i)
+                nc.gpsimd.memset(m_il[h][:].rearrange("p n t -> p (n t)").bitcast(U32), 0)
+            for h, (a, b) in enumerate(((SPAN, W), (0, 384))):
+                nc.gpsimd.memset(m_codes[h][:, a:b], 0)
+                nc.gpsimd.memset(m_scales[h][:, a:b].bitcast(U32), 0)
+            nc.gpsimd.memset(zeros[:], 0.0)
+            for step in ORDER:
+                name = step.split(":")[0]
+                engine = step.split(":")[1] if ":" in step else ""
+                d = [int(x) for x in name if x in "01234567"]
+                if name in ("CwA", "CwB"):
+                    load_cw(0 if name == "CwA" else 1)
+                elif name in ("G0", "G1"):
+                    nc.sync.dma_start(out=g_raw[d[0]][:], in_=g_v[d[0]])
+                elif name in ("x20", "x21"):
+                    nc.sync.dma_start(out=x2_raw[d[1]][:], in_=x2_v[d[1]])
+                elif name in ("z0", "z1"):
+                    nc.sync.dma_start(out=z_raw[d[0]][:], in_=z_v[d[0]])
+                elif name == "mask":
+                    load_mask()
+                elif name in ("T30", "T31"):
+                    load_t3(d[1])
+                elif name == "m1":
+                    load_mask_o()
+                elif name[:2] == "CI":
+                    cw_copy(d[0], {"A": 0, "B": 1}[name[3]], int(name[4]), engine)
+                elif name[:2] == "CQ":
+                    cw_quantize(d[0])
+                elif name[:2] == "GT":
+                    g_transpose(*d)
+                elif name[:2] == "GC":
+                    g_copy(*d)
+                elif name[:2] == "GQ":
+                    g_quantize(*d)
+                elif name[:2] == "DX":
+                    dx3(*d)
+                elif name[:2] == "MT":
+                    m_multiply(*d)
+                elif name[:2] == "MQ":
+                    if name[-1] == "a":
+                        m_quantize(d[0], 0, 512)
+                    else:
+                        m_quantize(d[0], 512, 128)
+                elif name[:2] == "TT":
+                    dpt_transpose(*d)
+                elif name[:2] == "TC":
+                    dpt_copy(*d)
+                elif name[:2] == "TQ":
+                    dpt_quantize(*d)
+                elif name[:2] == "OC":
+                    result_0(*d)
+                elif name[:2] == "OM":
+                    result_1(*d)
+                elif name[:2] == "ST":
+                    store_0(*d)
+                elif name[:2] == "SW":
+                    store_1(*d)
+                elif name[:2] == "ZR":
+                    zero_1(*d)
+                elif name[:2] == "ZI":
+                    z_copy(d[0], d[1], engine)
+                elif name[:2] == "ZQ":
+                    z_quantize(*d)
+                elif name[:2] == "AI":
+                    dpa_copy(d[0], d[1], engine)
+                elif name[:2] == "AQ":
+                    dpa_quantize(*d)
+                elif name[0] == "M":
+                    dp3(*d)
+                elif name[0] == "O":
+                    product_0(*d)
+                elif name[0] == "P":
+                    product_1(*d)
+                else:
+                    raise ValueError(step)

@@ -24,17 +24,19 @@ FLOPS = 2 * (B * O * K + 2 * B * K * W)
 BYTES = 2 * (4 * 1024 * 1024 + 2 * 512 * 1024) + 4 * 2 * 1024 * 1024
 
 ORDER = """
-G0 CwA CwB x20 G1 z1 m1 mask T30 GT01 GT00 GC01 GC00 T31 CI1A0:V CI1A1:V CI0A0:S GQ0 CI0A1:S z0
-CI1B1:V CI1B0:S CI0B1:V CI0B0:S CQ1 CQ0 DX031 ZR7 DX011 M031 DX001 M011 DX000 ZR1 GT10 M001 DX020
-GC10 M000 GT11 DX030 M020 GC11 DX010 TT00 M030 ZR4 ZI13:S x21 DX021 ZI10:V TT03 M010 TC00 ZR5 M021
-TC03 TT01 TQ00 AI00:S TT02 GQ1 ZR3 TC01 MT0 DX121 TC02 DX110 DX130 ZI12:S ZR0 AI07:S TQ02 MQ0a
-ZI11:S ZR6 ZQ11 MT1 ZI02:S ZR2 ZI00:S TQ01 AI01:S MQ1 MQ1a AI03:S MQ0 ZQ10 O021 AI05:S TQ03 O010
-OC021 M121 O031 OC010 M110 O000 OC031 M130 O020 OC000 ZI01:V O001 OC020 ZI03:V O030 OC001 ST02 ZQ00
-DX100 OC030 ST00 O011 ZQ01 ST03 DX111 OC011 DX131 M100 ST01 M111 DX101 M131 TT11 M101 DX120 TC11
-TT13 AI06:V TT10 TC13 TQ11 AI15:V O111 TC10 TQ13 O110 AI14:V OC111 TQ10 O131 OC110 AI16:V AI17:V
-O100 OC131 ST11 AI04:V O101 OC100 AQ11 O130 OC101 AQ01 OC130 ST10 M120 P7 ST13 AI02:V TT12 AI13:S
-OM7 P6 TC12 AQ00 SW7 P5 AI12:S OM6 P4 TQ12 AI10:S SW6 OM5 O121 AI11:S OM4 SW5 O120 SW4 OC121 AQ10
-OC120 P0 ST12 P1 OM0 P2 SW0 OM1 P3 SW1 OM2 SW2 OM3 SW3
+CwA CwB G0 T30 mask x20 T31 z0 x21 CI1A1:V CI0A1:S CI1A0:V CI0A0:V G1 CI0B0:V CI1B1:S CI0B1:V
+CI1B0:V m1 GT01 CQ0 GT00 CQ1 GC01:S ZR1 GC00:S ZR0 MK:S GQ0 MT01:V DX030 DX031 DX021 MT02:G ZR3 M030
+MT00:G M031 DX000 z1 M021 DX020 MT12:G TT03 M020 DX001 TC03:S MT11:G M000 TT02 DX011 M001 TC02:S
+DX010 ZR2 M011 ZI03:S TT00 M010 ZI02:S MT10:G TT01 TC00:S MQ0a TC01:S ZR5 TQ00 AI02:S MQ1 MQ1a ZR7
+AI05:S GT10 ZR4 TQ03 GT11 ZI07:S ZI05:V ZR6 MQ0 GC10:S TQ02 O030 AI01:V AI00:S O031 GC11:V AI06:G
+ZI06:S O020 GQ1 OC030:S ZI00:V DX121 OC020:S TQ01 DX111 OC031:S DX100 M121 ZI01:G O000 AI04:S M111
+ST03 ZI13:G DX120 O010 ZI11:S M100 ZI04:G DX101 M120 ZI14:S DX131 ZI12:G O021 M101 OC000:S TT12
+OC010:V AI03:G OC021:S TT10 M131 ZI15:S ST02 ZI16:G DX130 DX110 TC12:V TC10:S O011 AI07:G M130
+AI14:S O001 AI16:V AI15:S TT13 TQ12 ZI10:V OC011:S O120 ZQ01 OC001:S ST01 O121 TQ10 OC120:S ST00
+TC13:V O100 ZI17:S AQ01 O101 OC121:S TQ13 OC100:S ZQ11 ST12 O130 AI17:S AQ00 O131 OC130:S M110
+OC101:S AQ11 TT11 OC131:S ST10 ZQ00 P7 AI11:S ST13 ZQ10 P6 TC11:S OM7 AI10:G P4 AI12:S OM6 SW7 P5
+TQ11 AI13:S SW6 OM4 O110 OM5 SW4 O111 OC110:S AQ10 SW5 OC111:S P1 ST11 P2 OM1 P0 SW1 OM2 P3 SW2 OM0
+SW0 OM3 SW3
 """.split()
 
 
@@ -95,8 +97,12 @@ def tile_chebyshev_l3_sparsed32_stack_pb_v_kernel(
         def copy(engine, out, in_):
             if engine == "V":
                 nc.vector.tensor_copy(out=out, in_=in_)
-            else:
+            elif engine == "S":
                 nc.scalar.copy(out=out, in_=in_)
+            else:
+                nc.gpsimd.tensor_scalar(
+                    out=out, in0=in_, scalar1=1.0, scalar2=0.0, op0=MULT, op1=mybir.AluOpType.add
+                )
 
         def load_cw(c):
             nc.sync.dma_start(out=cw_raw[c][:], in_=cw_v[:, :, 512 * c : 512 * (c + 1)])
@@ -110,10 +116,10 @@ def tile_chebyshev_l3_sparsed32_stack_pb_v_kernel(
                 )
 
         def load_mask():
-            for u in range(2):
-                nc.sync.dma_start(
-                    out=mask_t[:, 2 * u : 2 * u + 2, 192 * u : 192 * u + WIN2], in_=mask_v[0, :, :, 0:WIN2]
-                )
+            nc.sync.dma_start(out=mask_t[:, 0:2, 0:WIN2], in_=mask_v[0, :, :, 0:WIN2])
+
+        def mask_copy(engine):
+            copy(engine, mask_t[:, 2:4, 192:SPAN], mask_t[:, 0:2, 0:WIN2])
 
         def load_mask_o():
             nc.sync.dma_start(out=mask_o[:], in_=mask_i[0, :, :, 0:WIN1])
@@ -140,8 +146,8 @@ def tile_chebyshev_l3_sparsed32_stack_pb_v_kernel(
                     nc.tensor.transpose(ps[:, a, u, :], words[:, u : O // 2 : 2], ident[:])
             psum["g", g, b] = ps
 
-        def g_copy(g, b):
-            copy("S", g_il[g][:, 2 * b : 2 * b + 2], psum["g", g, b][:].rearrange("p a u m -> p a m u"))
+        def g_copy(g, b, engine):
+            copy(engine, g_il[g][:, 2 * b : 2 * b + 2], psum["g", g, b][:].rearrange("p a u m -> p a m u"))
 
         def g_quantize(g):
             nc.vector.quantize_mx(
@@ -196,9 +202,9 @@ def tile_chebyshev_l3_sparsed32_stack_pb_v_kernel(
                     nc.tensor.transpose(ps[:, h, u, :], words[:, n : n + 128], ident[:])
             psum["dpt", g, t] = ps
 
-        def dpt_copy(g, t):
+        def dpt_copy(g, t, engine):
             il = stage.tile([P, 2, P, 2], F32, name="dpt_il", align_bytes=64)
-            copy("S", il[:], psum["dpt", g, t][:].rearrange("p h u m -> p h m u"))
+            copy(engine, il[:], psum["dpt", g, t][:].rearrange("p h u m -> p h m u"))
             sbuf["dpt", g, t] = il
 
         def dpt_quantize(g, t):
@@ -210,9 +216,13 @@ def tile_chebyshev_l3_sparsed32_stack_pb_v_kernel(
 
         def dpa_copy(g, i, engine):
             hu, lo = i // 2, i % 2
-            src = dp[g][:].rearrange("p t (c s l q i) -> p c l s q t i", c=4, s=16, l=2, q=2, i=4)
-            dst = dpa_il[g][:, 128 * i : 128 * (i + 1), :].rearrange("p (s q i) t -> p s q t i", s=16, q=2, i=4)
-            copy(engine, dst, src[:, hu, lo])
+            dst = dpa_il[g][:, 128 * i : 128 * (i + 1), :]
+            if engine == "G":
+                src = dp[g][:].rearrange("p t (c s l j) -> p c l s j t", c=4, s=16, l=2, j=8)
+                copy(engine, dst.rearrange("p (s j) t -> p s j t", j=8), src[:, hu, lo])
+            else:
+                src = dp[g][:].rearrange("p t (c s l q i) -> p c l s q t i", c=4, s=16, l=2, q=2, i=4)
+                copy(engine, dst.rearrange("p (s q i) t -> p s q t i", s=16, q=2, i=4), src[:, hu, lo])
 
         def dpa_quantize(g, h):
             n = slice(512 * h, 512 * (h + 1))
@@ -222,14 +232,14 @@ def tile_chebyshev_l3_sparsed32_stack_pb_v_kernel(
                 in_=dpa_il[g][:, n, :].rearrange("p n t -> p (n t)"),
             )
 
-        def m_multiply(h):
-            for a, b, t0, t1 in ((0, 192, 0, 2), (192, 448, 0, 4), (448, 640, 2, 4)):
-                nc.vector.tensor_tensor(
-                    out=m_il[h][:, a:b, t0:t1].rearrange("p (c i) t -> p c t i", i=4),
-                    in0=t3_raw[h][:, t0:t1, a:b].rearrange("p t (c i) -> p c t i", i=4),
-                    in1=mask_t[:, t0:t1, a:b].rearrange("p t (c i) -> p c t i", i=4),
-                    op=MULT,
-                )
+        def m_multiply(h, k, engine):
+            a, b, t0, t1 = ((0, 192, 0, 2), (192, 448, 0, 4), (448, 640, 2, 4))[k]
+            (nc.vector if engine == "V" else nc.gpsimd).tensor_tensor(
+                out=m_il[h][:, a:b, t0:t1].rearrange("p (c i) t -> p c t i", i=4),
+                in0=t3_raw[h][:, t0:t1, a:b].rearrange("p t (c i) -> p c t i", i=4),
+                in1=mask_t[:, t0:t1, a:b].rearrange("p t (c i) -> p c t i", i=4),
+                op=MULT,
+            )
 
         def m_quantize(h, a, n):
             col = 384 * h + a
@@ -240,7 +250,7 @@ def tile_chebyshev_l3_sparsed32_stack_pb_v_kernel(
             )
 
         def z_copy(g, b, engine):
-            n = slice(256 * b, 256 * (b + 1))
+            n = slice(128 * b, 128 * (b + 1))
             copy(
                 engine,
                 z_il[g][:, n, :].rearrange("p (c i) t -> p c t i", i=4),
@@ -269,11 +279,11 @@ def tile_chebyshev_l3_sparsed32_stack_pb_v_kernel(
                 )
             psum["o0", g, t, w] = ps
 
-        def result_0(g, t, w):
+        def result_0(g, t, w, engine):
             if ("res0", g, t) not in sbuf:
                 res0 = stage0.tile([P, W], F32, name="res0")
                 sbuf["res0", g, t] = res0
-            copy("S", sbuf["res0", g, t][:, 512 * w : 512 * (w + 1)], psum["o0", g, t, w][:])
+            copy(engine, sbuf["res0", g, t][:, 512 * w : 512 * (w + 1)], psum["o0", g, t, w][:])
 
         def window(i):
             return min(96 * i // 64 * 64, W - 512)
@@ -334,13 +344,15 @@ def tile_chebyshev_l3_sparsed32_stack_pb_v_kernel(
                 elif name[:2] == "GT":
                     g_transpose(*d)
                 elif name[:2] == "GC":
-                    g_copy(*d)
+                    g_copy(*d, engine)
                 elif name[:2] == "GQ":
                     g_quantize(*d)
                 elif name[:2] == "DX":
                     dx3(*d)
                 elif name[:2] == "MT":
-                    m_multiply(*d)
+                    m_multiply(*d, engine)
+                elif name == "MK":
+                    mask_copy(engine)
                 elif name[:2] == "MQ":
                     if name[-1] == "a":
                         m_quantize(d[0], 0, 512)
@@ -349,11 +361,11 @@ def tile_chebyshev_l3_sparsed32_stack_pb_v_kernel(
                 elif name[:2] == "TT":
                     dpt_transpose(*d)
                 elif name[:2] == "TC":
-                    dpt_copy(*d)
+                    dpt_copy(*d, engine)
                 elif name[:2] == "TQ":
                     dpt_quantize(*d)
                 elif name[:2] == "OC":
-                    result_0(*d)
+                    result_0(*d, engine)
                 elif name[:2] == "OM":
                     result_1(*d)
                 elif name[:2] == "ST":

from contextlib import ExitStack

import concourse.mybir as mybir
from concourse.masks import make_identity

F32 = mybir.dt.float32
BF16 = mybir.dt.bfloat16
U32 = mybir.dt.uint32
U8 = mybir.dt.uint8
E4M3 = mybir.dt.float8_e4m3fn_x4
E5M2 = mybir.dt.float8_e5m2_x4
MULT = mybir.AluOpType.mult
COPY = mybir.ActivationFunctionType.Copy

P = 128
B, O, K, W = 1024, 512, 1024, 1024
GROUPS = 2
T = 4
SPAN = 640
WIN2 = 448
WIN1 = 352

FLOPS = 2 * (B * O * K + 2 * B * K * W)
BYTES = 2 * (4 * 1024 * 1024 + 2 * 512 * 1024) + 4 * 2 * 1024 * 1024

ORDER = """
CwA CwB G0 T30 mask x20 T31 z0 x21 CI1A1:V CI0A1:S CI1A0:V CI0A0:V G1 CI0B0:V CI1B1:S CI0B1:V
CI1B0:V m1 GT01 CQ0 GT00 CQ1 GC01:S ZR1 GC00:S ZR0 MK:S GQ0 MT01:V DX030 DX031 DX021 MT02:G ZR3 M030
MT00:G M031 DX000 z1 M021 DX020 MT12:G TT03 M020 DX001 TC03:S MT11:G M000 TT02 DX011 M001 TC02:S
DX010 ZR2 M011 ZI03:S TT00 M010 ZI02:S MT10:G TT01 TC00:S MQ0a TC01:S ZR5 TQ00 AI02:S MQ1 MQ1a ZR7
AI05:S GT10 ZR4 TQ03 GT11 ZI07:S ZI05:V ZR6 MQ0 GC10:S TQ02 O030 AI01:V AI00:S O031 GC11:V AI06:G
ZI06:S O020 GQ1 OC030:S ZI00:V DX121 OC020:S TQ01 DX111 OC031:S DX100 M121 ZI01:G O000 AI04:S M111
ST03 ZI13:G DX120 O010 ZI11:S M100 ZI04:G DX101 M120 ZI14:S DX131 ZI12:G O021 M101 OC000:S TT12
OC010:V AI03:G OC021:S TT10 M131 ZI15:S ST02 ZI16:G DX130 DX110 TC12:V TC10:S O011 AI07:G M130
AI14:S O001 AI16:V AI15:S TT13 TQ12 ZI10:V OC011:S O120 ZQ01 OC001:S ST01 O121 TQ10 OC120:S ST00
TC13:V O100 ZI17:S AQ01 O101 OC121:S TQ13 OC100:S ZQ11 ST12 O130 AI17:S AQ00 O131 OC130:S M110
OC101:S AQ11 TT11 OC131:S ST10 ZQ00 P7 AI11:S ST13 ZQ10 P6 TC11:S OM7 AI10:G P4 AI12:S OM6 SW7 P5
TQ11 AI13:S SW6 OM4 O110 OM5 SW4 O111 OC110:S AQ10 SW5 OC111:S P1 ST11 P2 OM1 P0 SW1 OM2 P3 SW2 OM0
SW0 OM3 SW3
""".split()


def tile_chebyshev_l3_sparsed32_stack_pb_v_kernel(
    tc, z, T3, mask, x1, x2, C_w, C_b, p3, grad_out, out_0, out_1
):
    nc = tc.nc
    with ExitStack() as ctx:
        keep = ctx.enter_context(tc.tile_pool(name="keep", bufs=1))
        stage = ctx.enter_context(tc.tile_pool(name="stage", bufs=4))
        stage0 = ctx.enter_context(tc.tile_pool(name="stage0", bufs=5))
        psum_t = ctx.enter_context(tc.psum_pool(name="psum_t", bufs=2))
        psum_d = ctx.enter_context(tc.psum_pool(name="psum_d", bufs=3))
        psum_o = ctx.enter_context(tc.psum_pool(name="psum_o", bufs=3))

        cw_raw = [keep.tile([P, T, 512], BF16, name="cw_raw%d" % c) for c in range(2)]
        g_raw = [keep.tile([P, T, O], BF16, name="g_raw%d" % g) for g in range(GROUPS)]
        x2_raw = [keep.tile([P, T, K], BF16, name="x2_raw%d" % g) for g in range(GROUPS)]
        z_raw = [keep.tile([P, T, W], BF16, name="z_raw%d" % g) for g in range(GROUPS)]
        t3_raw = [keep.tile([P, T, SPAN], BF16, name="t3_raw%d" % h) for h in range(2)]
        mask_t = keep.tile([P, T, SPAN], BF16, name="mask_t")
        mask_o = keep.tile([P, WIN1], BF16, name="mask_o")
        ident = keep.tile([P, P], F32, name="ident")
        zeros = keep.tile([P, 672], F32, name="zeros")

        cw_il = keep.tile([P, 2, 512, T], BF16, name="cw_il", align_bytes=64)
        cw_codes = keep.tile([P, 2, 512], U32, name="cw_codes", align_bytes=64)
        cw_scales = keep.tile([P, 2, 512], U8, name="cw_scales", align_bytes=64)
        g_il = [keep.tile([P, T, P, 2], F32, name="g_il%d" % g, align_bytes=64) for g in range(GROUPS)]
        g_codes = [keep.tile([P, T, P], U32, name="g_codes%d" % g, align_bytes=64) for g in range(GROUPS)]
        g_scales = [keep.tile([P, T, P], U8, name="g_scales%d" % g, align_bytes=64) for g in range(GROUPS)]
        m_il = [keep.tile([P, SPAN, T], BF16, name="m_il%d" % h, align_bytes=64) for h in range(2)]
        m_codes = [keep.tile([P, W], U32, name="m_codes%d" % h, align_bytes=64) for h in range(2)]
        m_scales = [keep.tile([P, W], U8, name="m_scales%d" % h, align_bytes=64) for h in range(2)]
        dp = [keep.tile([P, T, K], BF16, name="dp%d" % g) for g in range(GROUPS)]
        dpt_codes = [keep.tile([P, T, 2, P], U32, name="dpt_codes%d" % g, align_bytes=64) for g in range(GROUPS)]
        dpt_scales = [keep.tile([P, T, 2, P], U8, name="dpt_scales%d" % g, align_bytes=64) for g in range(GROUPS)]
        dpa_il = [keep.tile([P, K, T], BF16, name="dpa_il%d" % g, align_bytes=64) for g in range(GROUPS)]
        dpa_codes = [keep.tile([P, K], U32, name="dpa_codes%d" % g, align_bytes=64) for g in range(GROUPS)]
        dpa_scales = [keep.tile([P, K], U8, name="dpa_scales%d" % g, align_bytes=64) for g in range(GROUPS)]
        z_il = [keep.tile([P, W, T], BF16, name="z_il%d" % g, align_bytes=64) for g in range(GROUPS)]
        z_codes = [keep.tile([P, W], U32, name="z_codes%d" % g, align_bytes=64) for g in range(GROUPS)]
        z_scales = [keep.tile([P, W], U8, name="z_scales%d" % g, align_bytes=64) for g in range(GROUPS)]

        cw_v = C_w.rearrange("(p j) k -> p j k", j=T)
        g_v = grad_out.rearrange("(g p j) o -> g p j o", g=GROUPS, j=T)
        x2_v = x2.rearrange("(g p j) k -> g p j k", g=GROUPS, j=T)
        z_v = z.rearrange("(g p j) w -> g p j w", g=GROUPS, j=T)
        t3_v = T3.rearrange("(s c r) w -> c s r w", s=16, c=4, r=16)
        mask_v = mask.rearrange("(s c r) w -> c s r w", s=16, c=4, r=16)
        mask_i = mask.rearrange("(s i j) w -> i s j w", s=16, i=8, j=8)
        out0_v = out_0.rearrange("(g p t) w -> g t p w", g=GROUPS, t=T)
        out1_v = out_1.rearrange("(s i j) w -> i s j w", s=16, i=8, j=8)

        psum = {}
        sbuf = {}

        def copy(engine, out, in_):
            if engine == "V":
                nc.vector.tensor_copy(out=out, in_=in_)
            elif engine == "S":
                nc.scalar.copy(out=out, in_=in_)
            else:
                nc.gpsimd.tensor_scalar(
                    out=out, in0=in_, scalar1=1.0, scalar2=0.0, op0=MULT, op1=mybir.AluOpType.add
                )

        def load_cw(c):
            nc.sync.dma_start(out=cw_raw[c][:], in_=cw_v[:, :, 512 * c : 512 * (c + 1)])

        def load_t3(h):
            for u in range(2):
                col = 192 * (2 * h + u)
                nc.sync.dma_start(
                    out=t3_raw[h][:, 2 * u : 2 * u + 2, 192 * u : 192 * u + WIN2],
                    in_=t3_v[2 * h + u, :, :, col : col + WIN2],
                )

        def load_mask():
            nc.sync.dma_start(out=mask_t[:, 0:2, 0:WIN2], in_=mask_v[0, :, :, 0:WIN2])

        def mask_copy(engine):
            copy(engine, mask_t[:, 2:4, 192:SPAN], mask_t[:, 0:2, 0:WIN2])

        def load_mask_o():
            nc.sync.dma_start(out=mask_o[:], in_=mask_i[0, :, :, 0:WIN1])

        def store_0(g, t):
            nc.sync.dma_start(out=out0_v[g, t], in_=sbuf["res0", g, t][:])

        def store_1(i):
            first = 96 * i
            nc.sync.dma_start(out=out1_v[i, :, :, first : first + WIN1], in_=sbuf["res1", i][:])

        def zero_1(i):
            left, right = 96 * i, 672 - 96 * i
            if left > 0:
                nc.sync.dma_start(out=out1_v[i, :, :, 0:left], in_=zeros[:, 0:left])
            if right > 0:
                nc.sync.dma_start(out=out1_v[i, :, :, left + WIN1 : W], in_=zeros[:, 0:right])

        def g_transpose(g, b):
            ps = psum_t.tile([P, 2, 2, P], F32, name="tp")
            for a in range(2):
                words = g_raw[g][:, 2 * b + a, :].bitcast(F32)
                for u in range(2):
                    nc.tensor.transpose(ps[:, a, u, :], words[:, u : O // 2 : 2], ident[:])
            psum["g", g, b] = ps

        def g_copy(g, b, engine):
            copy(engine, g_il[g][:, 2 * b : 2 * b + 2], psum["g", g, b][:].rearrange("p a u m -> p a m u"))

        def g_quantize(g):
            nc.vector.quantize_mx(
                out=g_codes[g][:].rearrange("p t m -> p (t m)").bitcast(E5M2),
                scales=g_scales[g][:].rearrange("p t m -> p (t m)"),
                in_=g_il[g][:].rearrange("p t m u -> p (t m u)").bitcast(BF16),
            )

        def cw_copy(h, c, u, engine):
            src = cw_raw[c][:].rearrange("p j (s h u r) -> p h u s r j", s=8, h=2, u=2, r=16)[:, h, u]
            dst = cw_il[:, h].rearrange("p (u s r) j -> p u s r j", u=2, s=16, r=16)[:, u, 8 * c : 8 * c + 8]
            if engine == "V":
                nc.vector.tensor_scalar(out=dst, in0=src, scalar1=2.0, scalar2=None, op0=MULT)
            else:
                nc.scalar.activation(out=dst, in_=src, func=COPY, scale=2.0)

        def cw_quantize(h):
            nc.vector.quantize_mx(
                out=cw_codes[:, h, :].bitcast(E4M3),
                scales=cw_scales[:, h, :],
                in_=cw_il[:, h].rearrange("p n j -> p (n j)"),
            )

        def dx3(g, t, h):
            ps = psum_d.tile([P, 512], F32, name="dx")
            nc.tensor.matmul_mx(
                out=ps[:],
                lhsT=g_codes[g][:, t, :].bitcast(E5M2),
                lhsT_scale=g_scales[g][:, t, :],
                rhs=cw_codes[:, h, :].bitcast(E4M3),
                rhs_scale=cw_scales[:, h, :],
                start=True,
                stop=True,
            )
            psum["dx", g, t, h] = ps

        def dp3(g, t, h):
            x2_p = x2_raw[g][:, t, :].rearrange("p (s h u r) -> p h u s r", s=16, h=2, u=2, r=16)
            nc.vector.tensor_tensor(
                out=dp[g][:, t, 512 * h : 512 * (h + 1)].rearrange("p (u s r) -> p u s r", u=2, r=16),
                in0=psum["dx", g, t, h][:].rearrange("p (u s r) -> p u s r", u=2, r=16),
                in1=x2_p[:, h],
                op=MULT,
            )

        def dpt_transpose(g, t):
            ps = psum_t.tile([P, 2, 2, P], F32, name="tp")
            words = dp[g][:, t, :].bitcast(F32)
            for h in range(2):
                for u in range(2):
                    n = 128 * (2 * h + u)
                    nc.tensor.transpose(ps[:, h, u, :], words[:, n : n + 128], ident[:])
            psum["dpt", g, t] = ps

        def dpt_copy(g, t, engine):
            il = stage.tile([P, 2, P, 2], F32, name="dpt_il", align_bytes=64)
            copy(engine, il[:], psum["dpt", g, t][:].rearrange("p h u m -> p h m u"))
            sbuf["dpt", g, t] = il

        def dpt_quantize(g, t):
            nc.vector.quantize_mx(
                out=dpt_codes[g][:, t].rearrange("p h m -> p (h m)").bitcast(E5M2),
                scales=dpt_scales[g][:, t].rearrange("p h m -> p (h m)"),
                in_=sbuf["dpt", g, t][:].rearrange("p h m u -> p (h m u)").bitcast(BF16),
            )

        def dpa_copy(g, i, engine):
            hu, lo = i // 2, i % 2
            dst = dpa_il[g][:, 128 * i : 128 * (i + 1), :]
            if engine == "G":
                src = dp[g][:].rearrange("p t (c s l j) -> p c l s j t", c=4, s=16, l=2, j=8)
                copy(engine, dst.rearrange("p (s j) t -> p s j t", j=8), src[:, hu, lo])
            else:
                src = dp[g][:].rearrange("p t (c s l q i) -> p c l s q t i", c=4, s=16, l=2, q=2, i=4)
                copy(engine, dst.rearrange("p (s q i) t -> p s q t i", s=16, q=2, i=4), src[:, hu, lo])

        def dpa_quantize(g, h):
            n = slice(512 * h, 512 * (h + 1))
            nc.vector.quantize_mx(
                out=dpa_codes[g][:, n].bitcast(E5M2),
                scales=dpa_scales[g][:, n],
                in_=dpa_il[g][:, n, :].rearrange("p n t -> p (n t)"),
            )

        def m_multiply(h, k, engine):
            a, b, t0, t1 = ((0, 192, 0, 2), (192, 448, 0, 4), (448, 640, 2, 4))[k]
            (nc.vector if engine == "V" else nc.gpsimd).tensor_tensor(
                out=m_il[h][:, a:b, t0:t1].rearrange("p (c i) t -> p c t i", i=4),
                in0=t3_raw[h][:, t0:t1, a:b].rearrange("p t (c i) -> p c t i", i=4),
                in1=mask_t[:, t0:t1, a:b].rearrange("p t (c i) -> p c t i", i=4),
                op=MULT,
            )

        def m_quantize(h, a, n):
            col = 384 * h + a
            nc.vector.quantize_mx(
                out=m_codes[h][:, col : col + n].bitcast(E4M3),
                scales=m_scales[h][:, col : col + n],
                in_=m_il[h][:, a : a + n, :].rearrange("p n t -> p (n t)"),
            )

        def z_copy(g, b, engine):
            n = slice(128 * b, 128 * (b + 1))
            copy(
                engine,
                z_il[g][:, n, :].rearrange("p (c i) t -> p c t i", i=4),
                z_raw[g][:, :, n].rearrange("p t (c i) -> p c t i", i=4),
            )

        def z_quantize(g, b):
            n = slice(512 * b, 512 * (b + 1))
            nc.vector.quantize_mx(
                out=z_codes[g][:, n].bitcast(E4M3),
                scales=z_scales[g][:, n],
                in_=z_il[g][:, n, :].rearrange("p n t -> p (n t)"),
            )

        def product_0(g, t, w):
            ps = psum_o.tile([P, 512], F32, name="po")
            for h in range(2):
                nc.tensor.matmul_mx(
                    out=ps[:],
                    lhsT=dpt_codes[g][:, t, h, :].bitcast(E5M2),
                    lhsT_scale=dpt_scales[g][:, t, h, :],
                    rhs=m_codes[h][:, 512 * w : 512 * (w + 1)].bitcast(E4M3),
                    rhs_scale=m_scales[h][:, 512 * w : 512 * (w + 1)],
                    start=(h == 0),
                    stop=(h == 1),
                )
            psum["o0", g, t, w] = ps

        def result_0(g, t, w, engine):
            if ("res0", g, t) not in sbuf:
                res0 = stage0.tile([P, W], F32, name="res0")
                sbuf["res0", g, t] = res0
            copy(engine, sbuf["res0", g, t][:, 512 * w : 512 * (w + 1)], psum["o0", g, t, w][:])

        def window(i):
            return min(96 * i // 64 * 64, W - 512)

        def product_1(i):
            base = window(i)
            ps = psum_o.tile([P, 512], F32, name="po")
            for g in range(GROUPS):
                nc.tensor.matmul_mx(
                    out=ps[:],
                    lhsT=dpa_codes[g][:, 128 * i : 128 * (i + 1)].bitcast(E5M2),
                    lhsT_scale=dpa_scales[g][:, 128 * i : 128 * (i + 1)],
                    rhs=z_codes[g][:, base : base + 512].bitcast(E4M3),
                    rhs_scale=z_scales[g][:, base : base + 512],
                    start=(g == 0),
                    stop=(g == GROUPS - 1),
                )
            psum["o1", i] = ps

        def result_1(i):
            first = 96 * i - window(i)
            res1 = stage.tile([P, WIN1], F32, name="res1")
            nc.vector.tensor_tensor(
                out=res1[:], in0=psum["o1", i][:, first : first + WIN1], in1=mask_o[:], op=MULT
            )
            sbuf["res1", i] = res1

        with tc.manual_schedule():
            make_identity(nc, ident[:])
            for h in range(2):
                nc.gpsimd.memset(m_il[h][:].rearrange("p n t -> p (n t)").bitcast(U32), 0)
            for h, (a, b) in enumerate(((SPAN, W), (0, 384))):
                nc.gpsimd.memset(m_codes[h][:, a:b], 0)
                nc.gpsimd.memset(m_scales[h][:, a:b].bitcast(U32), 0)
            nc.gpsimd.memset(zeros[:], 0.0)
            for step in ORDER:
                name = step.split(":")[0]
                engine = step.split(":")[1] if ":" in step else ""
                d = [int(x) for x in name if x in "01234567"]
                if name in ("CwA", "CwB"):
                    load_cw(0 if name == "CwA" else 1)
                elif name in ("G0", "G1"):
                    nc.sync.dma_start(out=g_raw[d[0]][:], in_=g_v[d[0]])
                elif name in ("x20", "x21"):
                    nc.sync.dma_start(out=x2_raw[d[1]][:], in_=x2_v[d[1]])
                elif name in ("z0", "z1"):
                    nc.sync.dma_start(out=z_raw[d[0]][:], in_=z_v[d[0]])
                elif name == "mask":
                    load_mask()
                elif name in ("T30", "T31"):
                    load_t3(d[1])
                elif name == "m1":
                    load_mask_o()
                elif name[:2] == "CI":
                    cw_copy(d[0], {"A": 0, "B": 1}[name[3]], int(name[4]), engine)
                elif name[:2] == "CQ":
                    cw_quantize(d[0])
                elif name[:2] == "GT":
                    g_transpose(*d)
                elif name[:2] == "GC":
                    g_copy(*d, engine)
                elif name[:2] == "GQ":
                    g_quantize(*d)
                elif name[:2] == "DX":
                    dx3(*d)
                elif name[:2] == "MT":
                    m_multiply(*d, engine)
                elif name == "MK":
                    mask_copy(engine)
                elif name[:2] == "MQ":
                    if name[-1] == "a":
                        m_quantize(d[0], 0, 512)
                    else:
                        m_quantize(d[0], 512, 128)
                elif name[:2] == "TT":
                    dpt_transpose(*d)
                elif name[:2] == "TC":
                    dpt_copy(*d, engine)
                elif name[:2] == "TQ":
                    dpt_quantize(*d)
                elif name[:2] == "OC":
                    result_0(*d, engine)
                elif name[:2] == "OM":
                    result_1(*d)
                elif name[:2] == "ST":
                    store_0(*d)
                elif name[:2] == "SW":
                    store_1(*d)
                elif name[:2] == "ZR":
                    zero_1(*d)
                elif name[:2] == "ZI":
                    z_copy(d[0], d[1], engine)
                elif name[:2] == "ZQ":
                    z_quantize(*d)
                elif name[:2] == "AI":
                    dpa_copy(d[0], d[1], engine)
                elif name[:2] == "AQ":
                    dpa_quantize(*d)
                elif name[0] == "M":
                    dp3(*d)
                elif name[0] == "O":
                    product_0(*d)
                elif name[0] == "P":
                    product_1(*d)
                else:
                    raise ValueError(step)
